import numpy as np
import ml_dtypes

BF16 = ml_dtypes.bfloat16


def bf(x):
    return np.asarray(x, np.float32).astype(BF16)


def f32(x):
    return np.asarray(x, np.float32)


def f64(x):
    return np.asarray(x).astype(np.float64)


def striped(idx):
    return np.tile(idx.reshape(-1, 16).T, (8, 1))


C, S, N = 384, 4096, 2048
P = 0.5


def setup_inputs():
    return {"x": f32(np.abs(np.random.standard_normal((C, S)))), "keep": f32(np.random.random((C, N)) >= P), "offs": striped(np.random.permutation(S)[:N])}


def reference(x, keep, offs):
    idx = offs[:16].T.reshape(-1)
    sub = f64(x)[:, idx]
    zeroed = sub * f64(keep)
    comp = (sub.sum(axis=1, keepdims=True) - zeroed.sum(axis=1, keepdims=True)) / N
    return zeroed + comp

@@ -1,0 +1,47 @@
+import concourse.mybir as mybir
+
+F32 = mybir.dt.float32
+U16 = mybir.dt.uint16
+MULT = mybir.AluOpType.mult
+COPY = mybir.ActivationFunctionType.Copy
+IDENTITY = mybir.ActivationFunctionType.Identity
+
+P = 128
+ROWS, CHANNELS, PICKED = 384, 4096, 2048
+BLOCKS = ROWS // P
+
+
+def tile_dropout_partial_binary_kernel(tc, x, keep, offs, out):
+    nc = tc.nc
+    with (
+        tc.tile_pool(name="held", bufs=1) as held,
+        tc.tile_pool(name="blocks", bufs=BLOCKS) as blocks,
+    ):
+        offsets = held.tile([P, PICKED // 16], U16, name="offsets")
+        nc.sync.dma_start(offsets[:], offs)
+
+        kept_masks, windows = [], []
+        for b in range(BLOCKS):
+            rows = slice(b * P, (b + 1) * P)
+            kept_mask = blocks.tile([P, PICKED], F32, name="kept_mask")
+            nc.sync.dma_start(kept_mask[:], keep[rows, :])
+            window = blocks.tile([P, CHANNELS], F32, name="window")
+            nc.sync.dma_start(window[:], x[rows, :])
+            kept_masks.append(kept_mask)
+            windows.append(window)
+
+        for b in range(BLOCKS):
+            rows = slice(b * P, (b + 1) * P)
+            kept_mask, window = kept_masks[b], windows[b]
+
+            dropped_mask = blocks.tile([P, PICKED], F32, name="dropped_mask")
+            nc.scalar.activation(dropped_mask[:], kept_mask[:], COPY, bias=1.0, scale=-1.0)
+            dropped = blocks.tile([P, PICKED], F32, name="dropped")
+            nc.vector.tensor_tensor(dropped[:], window[:].indirect(offsets[:]), dropped_mask[:], MULT)
+            comp = blocks.tile([P, 1], F32, name="comp")
+            nc.scalar.activation(dropped[:], dropped[:], COPY, scale=1.0 / PICKED, accum_out=comp[:])
+
+            result = blocks.tile([P, PICKED], F32, name="result")
+            nc.vector.tensor_tensor(result[:], window[:].indirect(offsets[:]), kept_mask[:], MULT)
+            nc.scalar.activation(result[:], result[:], IDENTITY, bias=comp[:])
+            nc.sync.dma_start(out[rows, :], result[:])

@@ -9,6 +9,7 @@ IDENTITY = mybir.ActivationFunctionType.Identity
 P = 128
 ROWS, CHANNELS, PICKED = 384, 4096, 2048
 BLOCKS = ROWS // P
+PIECE = 512
 
 
 def tile_dropout_partial_binary_kernel(tc, x, keep, offs, out):
@@ -16,6 +17,7 @@ def tile_dropout_partial_binary_kernel(tc, x, keep, offs, out):
     with (
         tc.tile_pool(name="held", bufs=1) as held,
         tc.tile_pool(name="blocks", bufs=BLOCKS) as blocks,
+        tc.tile_pool(name="pieces", bufs=4) as pieces,
     ):
         offsets = held.tile([P, PICKED // 16], U16, name="offsets")
         nc.sync.dma_start(offsets[:], offs)
@@ -41,7 +43,10 @@ def tile_dropout_partial_binary_kernel(tc, x, keep, offs, out):
             comp = blocks.tile([P, 1], F32, name="comp")
             nc.scalar.activation(dropped[:], dropped[:], COPY, scale=1.0 / PICKED, accum_out=comp[:])
 
-            result = blocks.tile([P, PICKED], F32, name="result")
-            nc.vector.tensor_tensor(result[:], window[:].indirect(offsets[:]), kept_mask[:], MULT)
-            nc.scalar.activation(result[:], result[:], IDENTITY, bias=comp[:])
-            nc.sync.dma_start(out[rows, :], result[:])
+            for first in range(0, PICKED, PIECE):
+                cols = slice(first, first + PIECE)
+                result = pieces.tile([P, PIECE], F32, name="result")
+                looked_up = window[:].indirect(offsets[:, first // 16 : (first + PIECE) // 16])
+                nc.vector.tensor_tensor(result[:], looked_up, kept_mask[:, cols], MULT)
+                nc.scalar.activation(result[:], result[:], IDENTITY, bias=comp[:])
+                nc.sync.dma_start(out[rows, cols], result[:])

@@ -17,36 +17,36 @@ def tile_dropout_partial_binary_kernel(tc, x, keep, offs, out):
     with (
         tc.tile_pool(name="held", bufs=1) as held,
         tc.tile_pool(name="blocks", bufs=BLOCKS) as blocks,
-        tc.tile_pool(name="pieces", bufs=4) as pieces,
     ):
         offsets = held.tile([P, PICKED // 16], U16, name="offsets")
         nc.sync.dma_start(offsets[:], offs)
 
-        kept_masks, windows = [], []
+        kept_masks, dropped_masks, windows = [], [], []
         for b in range(BLOCKS):
             rows = slice(b * P, (b + 1) * P)
             kept_mask = blocks.tile([P, PICKED], F32, name="kept_mask")
             nc.sync.dma_start(kept_mask[:], keep[rows, :])
             window = blocks.tile([P, CHANNELS], F32, name="window")
             nc.sync.dma_start(window[:], x[rows, :])
+            dropped_mask = blocks.tile([P, PICKED], F32, name="dropped_mask")
+            nc.scalar.activation(dropped_mask[:], kept_mask[:], COPY, bias=1.0, scale=-1.0)
             kept_masks.append(kept_mask)
+            dropped_masks.append(dropped_mask)
             windows.append(window)
 
         for b in range(BLOCKS):
             rows = slice(b * P, (b + 1) * P)
-            kept_mask, window = kept_masks[b], windows[b]
+            kept_mask, dropped_mask, window = kept_masks[b], dropped_masks[b], windows[b]
 
-            dropped_mask = blocks.tile([P, PICKED], F32, name="dropped_mask")
-            nc.scalar.activation(dropped_mask[:], kept_mask[:], COPY, bias=1.0, scale=-1.0)
             dropped = blocks.tile([P, PICKED], F32, name="dropped")
             nc.vector.tensor_tensor(dropped[:], window[:].indirect(offsets[:]), dropped_mask[:], MULT)
             comp = blocks.tile([P, 1], F32, name="comp")
             nc.scalar.activation(dropped[:], dropped[:], COPY, scale=1.0 / PICKED, accum_out=comp[:])
 
+            result = blocks.tile([P, PICKED], F32, name="result")
             for first in range(0, PICKED, PIECE):
                 cols = slice(first, first + PIECE)
-                result = pieces.tile([P, PIECE], F32, name="result")
                 looked_up = window[:].indirect(offsets[:, first // 16 : (first + PIECE) // 16])
-                nc.vector.tensor_tensor(result[:], looked_up, kept_mask[:, cols], MULT)
-                nc.scalar.activation(result[:], result[:], IDENTITY, bias=comp[:])
-                nc.sync.dma_start(out[rows, cols], result[:])
+                nc.vector.tensor_tensor(result[:, cols], looked_up, kept_mask[:, cols], MULT)
+                nc.scalar.activation(result[:, cols], result[:, cols], IDENTITY, bias=comp[:])
+                nc.scalar.dma_start(out[rows, cols], result[:, cols])

@@ -10,6 +10,7 @@ P = 128
 ROWS, CHANNELS, PICKED = 384, 4096, 2048
 BLOCKS = ROWS // P
 PIECE = 512
+FIRSTS = range(0, PICKED, PIECE)
 
 
 def tile_dropout_partial_binary_kernel(tc, x, keep, offs, out):
@@ -21,32 +22,43 @@ def tile_dropout_partial_binary_kernel(tc, x, keep, offs, out):
         offsets = held.tile([P, PICKED // 16], U16, name="offsets")
         nc.sync.dma_start(offsets[:], offs)
 
-        kept_masks, dropped_masks, windows = [], [], []
-        for b in range(BLOCKS):
-            rows = slice(b * P, (b + 1) * P)
-            kept_mask = blocks.tile([P, PICKED], F32, name="kept_mask")
-            nc.sync.dma_start(kept_mask[:], keep[rows, :])
-            window = blocks.tile([P, CHANNELS], F32, name="window")
-            nc.sync.dma_start(window[:], x[rows, :])
-            dropped_mask = blocks.tile([P, PICKED], F32, name="dropped_mask")
-            nc.scalar.activation(dropped_mask[:], kept_mask[:], COPY, bias=1.0, scale=-1.0)
-            kept_masks.append(kept_mask)
-            dropped_masks.append(dropped_mask)
-            windows.append(window)
+        def looked_up(window, first):
+            return window[:].indirect(offsets[:, first // 16 : (first + PIECE) // 16])
+
+        kept_masks = [blocks.tile([P, PICKED], F32, name="kept_mask") for b in range(BLOCKS)]
+        dropped_masks = [blocks.tile([P, PICKED], F32, name="dropped_mask") for b in range(BLOCKS)]
+        windows = [blocks.tile([P, CHANNELS], F32, name="window") for b in range(BLOCKS)]
+
+        def load_window(b):
+            nc.sync.dma_start(windows[b][:], x[b * P : (b + 1) * P, :])
+
+        def load_masks(b, firsts):
+            for first in firsts:
+                cols = slice(first, first + PIECE)
+                nc.sync.dma_start(kept_masks[b][:, cols], keep[b * P : (b + 1) * P, cols])
+                nc.scalar.activation(dropped_masks[b][:, cols], kept_masks[b][:, cols], COPY, bias=1.0, scale=-1.0)
+
+        load_masks(0, FIRSTS[:1])
+        load_window(0)
+        load_masks(0, FIRSTS[1:])
+        for b in range(1, BLOCKS):
+            load_masks(b, FIRSTS)
+            load_window(b)
 
         for b in range(BLOCKS):
             rows = slice(b * P, (b + 1) * P)
             kept_mask, dropped_mask, window = kept_masks[b], dropped_masks[b], windows[b]
 
             dropped = blocks.tile([P, PICKED], F32, name="dropped")
-            nc.vector.tensor_tensor(dropped[:], window[:].indirect(offsets[:]), dropped_mask[:], MULT)
+            for first in FIRSTS:
+                cols = slice(first, first + PIECE)
+                nc.vector.tensor_tensor(dropped[:, cols], looked_up(window, first), dropped_mask[:, cols], MULT)
             comp = blocks.tile([P, 1], F32, name="comp")
             nc.scalar.activation(dropped[:], dropped[:], COPY, scale=1.0 / PICKED, accum_out=comp[:])
 
             result = blocks.tile([P, PICKED], F32, name="result")
-            for first in range(0, PICKED, PIECE):
+            for first in FIRSTS:
                 cols = slice(first, first + PIECE)
-                looked_up = window[:].indirect(offsets[:, first // 16 : (first + PIECE) // 16])
-                nc.vector.tensor_tensor(result[:, cols], looked_up, kept_mask[:, cols], MULT)
+                nc.vector.tensor_tensor(result[:, cols], looked_up(window, first), kept_mask[:, cols], MULT)
                 nc.scalar.activation(result[:, cols], result[:, cols], IDENTITY, bias=comp[:])
                 nc.scalar.dma_start(out[rows, cols], result[:, cols])

@@ -9,8 +9,14 @@ IDENTITY = mybir.ActivationFunctionType.Identity
 P = 128
 ROWS, CHANNELS, PICKED = 384, 4096, 2048
 BLOCKS = ROWS // P
-PIECE = 512
-FIRSTS = range(0, PICKED, PIECE)
+QUARTER = PICKED // 4
+QUARTERS = [QUARTER] * 4
+WHOLE = [PICKED]
+HALVING = [1024, 512, 256, 128, 128]
+
+
+def pieces(widths):
+    return [slice(sum(widths[:i]), sum(widths[: i + 1])) for i in range(len(widths))]
 
 
 def tile_dropout_partial_binary_kernel(tc, x, keep, offs, out):
@@ -22,8 +28,8 @@ def tile_dropout_partial_binary_kernel(tc, x, keep, offs, out):
         offsets = held.tile([P, PICKED // 16], U16, name="offsets")
         nc.sync.dma_start(offsets[:], offs)
 
-        def looked_up(window, first):
-            return window[:].indirect(offsets[:, first // 16 : (first + PIECE) // 16])
+        def looked_up(window, cols):
+            return window[:].indirect(offsets[:, cols.start // 16 : cols.stop // 16])
 
         kept_masks = [blocks.tile([P, PICKED], F32, name="kept_mask") for b in range(BLOCKS)]
         dropped_masks = [blocks.tile([P, PICKED], F32, name="dropped_mask") for b in range(BLOCKS)]
@@ -32,33 +38,33 @@ def tile_dropout_partial_binary_kernel(tc, x, keep, offs, out):
         def load_window(b):
             nc.sync.dma_start(windows[b][:], x[b * P : (b + 1) * P, :])
 
-        def load_masks(b, firsts):
-            for first in firsts:
-                cols = slice(first, first + PIECE)
+        def load_masks(b, quarters):
+            for cols in quarters:
                 nc.sync.dma_start(kept_masks[b][:, cols], keep[b * P : (b + 1) * P, cols])
                 nc.scalar.activation(dropped_masks[b][:, cols], kept_masks[b][:, cols], COPY, bias=1.0, scale=-1.0)
 
-        load_masks(0, FIRSTS[:1])
+        load_masks(0, pieces(QUARTERS)[:1])
         load_window(0)
-        load_masks(0, FIRSTS[1:])
+        load_masks(0, pieces(QUARTERS)[1:])
         for b in range(1, BLOCKS):
-            load_masks(b, FIRSTS)
+            load_masks(b, pieces(QUARTERS))
             load_window(b)
 
         for b in range(BLOCKS):
             rows = slice(b * P, (b + 1) * P)
             kept_mask, dropped_mask, window = kept_masks[b], dropped_masks[b], windows[b]
 
+            dropped_pieces = pieces(QUARTERS if b == 0 else WHOLE)
+            kept_pieces = pieces(HALVING if b == BLOCKS - 1 else WHOLE)
+
             dropped = blocks.tile([P, PICKED], F32, name="dropped")
-            for first in FIRSTS:
-                cols = slice(first, first + PIECE)
-                nc.vector.tensor_tensor(dropped[:, cols], looked_up(window, first), dropped_mask[:, cols], MULT)
+            for cols in dropped_pieces:
+                nc.vector.tensor_tensor(dropped[:, cols], looked_up(window, cols), dropped_mask[:, cols], MULT)
             comp = blocks.tile([P, 1], F32, name="comp")
             nc.scalar.activation(dropped[:], dropped[:], COPY, scale=1.0 / PICKED, accum_out=comp[:])
 
             result = blocks.tile([P, PICKED], F32, name="result")
-            for first in FIRSTS:
-                cols = slice(first, first + PIECE)
-                nc.vector.tensor_tensor(result[:, cols], looked_up(window, first), kept_mask[:, cols], MULT)
+            for cols in kept_pieces:
+                nc.vector.tensor_tensor(result[:, cols], looked_up(window, cols), kept_mask[:, cols], MULT)
                 nc.scalar.activation(result[:, cols], result[:, cols], IDENTITY, bias=comp[:])
                 nc.scalar.dma_start(out[rows, cols], result[:, cols])

@@ -9,9 +9,8 @@ IDENTITY = mybir.ActivationFunctionType.Identity
 P = 128
 ROWS, CHANNELS, PICKED = 384, 4096, 2048
 BLOCKS = ROWS // P
-QUARTER = PICKED // 4
-QUARTERS = [QUARTER] * 4
 WHOLE = [PICKED]
+RISING = [128, 384, 512, 1024]
 HALVING = [1024, 512, 256, 128, 128]
 
 
@@ -28,43 +27,49 @@ def tile_dropout_partial_binary_kernel(tc, x, keep, offs, out):
         offsets = held.tile([P, PICKED // 16], U16, name="offsets")
         nc.sync.dma_start(offsets[:], offs)
 
-        def looked_up(window, cols):
-            return window[:].indirect(offsets[:, cols.start // 16 : cols.stop // 16])
-
         kept_masks = [blocks.tile([P, PICKED], F32, name="kept_mask") for b in range(BLOCKS)]
         dropped_masks = [blocks.tile([P, PICKED], F32, name="dropped_mask") for b in range(BLOCKS)]
         windows = [blocks.tile([P, CHANNELS], F32, name="window") for b in range(BLOCKS)]
+        droppeds = [blocks.tile([P, PICKED], F32, name="dropped") for b in range(BLOCKS)]
+        comps = [blocks.tile([P, 1], F32, name="comp") for b in range(BLOCKS)]
+        results = [blocks.tile([P, PICKED], F32, name="result") for b in range(BLOCKS)]
 
         def load_window(b):
             nc.sync.dma_start(windows[b][:], x[b * P : (b + 1) * P, :])
 
-        def load_masks(b, quarters):
-            for cols in quarters:
+        def load_masks(b, cuts):
+            for cols in cuts:
                 nc.sync.dma_start(kept_masks[b][:, cols], keep[b * P : (b + 1) * P, cols])
                 nc.scalar.activation(dropped_masks[b][:, cols], kept_masks[b][:, cols], COPY, bias=1.0, scale=-1.0)
 
-        load_masks(0, pieces(QUARTERS)[:1])
+        def looked_up(b, cols):
+            return windows[b][:].indirect(offsets[:, cols.start // 16 : cols.stop // 16])
+
+        def share_of_lost_mass(b):
+            nc.vector.tensor_tensor(droppeds[b][:], looked_up(b, slice(0, PICKED)), dropped_masks[b][:], MULT)
+            nc.scalar.activation(droppeds[b][:], droppeds[b][:], COPY, scale=1.0 / PICKED, accum_out=comps[b][:])
+
+        def zero_the_dropped(b, cols):
+            nc.vector.tensor_tensor(results[b][:, cols], looked_up(b, cols), kept_masks[b][:, cols], MULT)
+
+        def add_share_and_store(b, cols):
+            nc.scalar.activation(results[b][:, cols], results[b][:, cols], IDENTITY, bias=comps[b][:])
+            nc.scalar.dma_start(out[b * P : (b + 1) * P, cols], results[b][:, cols])
+
+        load_masks(0, pieces(RISING)[:1])
         load_window(0)
-        load_masks(0, pieces(QUARTERS)[1:])
+        load_masks(0, pieces(RISING)[1:])
         for b in range(1, BLOCKS):
-            load_masks(b, pieces(QUARTERS))
+            load_masks(b, pieces(WHOLE))
             load_window(b)
 
-        for b in range(BLOCKS):
-            rows = slice(b * P, (b + 1) * P)
-            kept_mask, dropped_mask, window = kept_masks[b], dropped_masks[b], windows[b]
+        for cols in pieces(RISING):
+            zero_the_dropped(0, cols)
+        share_of_lost_mass(0)
+        add_share_and_store(0, slice(0, PICKED))
 
-            dropped_pieces = pieces(QUARTERS if b == 0 else WHOLE)
-            kept_pieces = pieces(HALVING if b == BLOCKS - 1 else WHOLE)
-
-            dropped = blocks.tile([P, PICKED], F32, name="dropped")
-            for cols in dropped_pieces:
-                nc.vector.tensor_tensor(dropped[:, cols], looked_up(window, cols), dropped_mask[:, cols], MULT)
-            comp = blocks.tile([P, 1], F32, name="comp")
-            nc.scalar.activation(dropped[:], dropped[:], COPY, scale=1.0 / PICKED, accum_out=comp[:])
-
-            result = blocks.tile([P, PICKED], F32, name="result")
-            for cols in kept_pieces:
-                nc.vector.tensor_tensor(result[:, cols], looked_up(window, cols), kept_mask[:, cols], MULT)
-                nc.scalar.activation(result[:, cols], result[:, cols], IDENTITY, bias=comp[:])
-                nc.scalar.dma_start(out[rows, cols], result[:, cols])
+        for b in range(1, BLOCKS):
+            share_of_lost_mass(b)
+            for cols in pieces(HALVING if b == BLOCKS - 1 else WHOLE):
+                zero_the_dropped(b, cols)
+                add_share_and_store(b, cols)

@@ -11,7 +11,7 @@ ROWS, CHANNELS, PICKED = 384, 4096, 2048
 BLOCKS = ROWS // P
 WHOLE = [PICKED]
 RISING = [128, 384, 512, 1024]
-HALVING = [1024, 512, 256, 128, 128]
+TAPER = [832, 576, 384, 256]
 
 
 def pieces(widths):
@@ -70,6 +70,6 @@ def tile_dropout_partial_binary_kernel(tc, x, keep, offs, out):
 
         for b in range(1, BLOCKS):
             share_of_lost_mass(b)
-            for cols in pieces(HALVING if b == BLOCKS - 1 else WHOLE):
+            for cols in pieces(TAPER if b == BLOCKS - 1 else WHOLE):
                 zero_the_dropped(b, cols)
                 add_share_and_store(b, cols)

@@ -52,9 +52,9 @@ def tile_dropout_partial_binary_kernel(tc, x, keep, offs, out):
         def zero_the_dropped(b, cols):
             nc.vector.tensor_tensor(results[b][:, cols], looked_up(b, cols), kept_masks[b][:, cols], MULT)
 
-        def add_share_and_store(b, cols):
+        def add_share_and_store(b, cols, store_queue):
             nc.scalar.activation(results[b][:, cols], results[b][:, cols], IDENTITY, bias=comps[b][:])
-            nc.scalar.dma_start(out[b * P : (b + 1) * P, cols], results[b][:, cols])
+            store_queue.dma_start(out[b * P : (b + 1) * P, cols], results[b][:, cols])
 
         load_masks(0, pieces(RISING)[:1])
         load_window(0)
@@ -66,10 +66,12 @@ def tile_dropout_partial_binary_kernel(tc, x, keep, offs, out):
         for cols in pieces(RISING):
             zero_the_dropped(0, cols)
         share_of_lost_mass(0)
-        add_share_and_store(0, slice(0, PICKED))
+        add_share_and_store(0, slice(0, PICKED), nc.scalar)
 
-        for b in range(1, BLOCKS):
-            share_of_lost_mass(b)
-            for cols in pieces(TAPER if b == BLOCKS - 1 else WHOLE):
-                zero_the_dropped(b, cols)
-                add_share_and_store(b, cols)
+        share_of_lost_mass(1)
+        zero_the_dropped(1, slice(0, PICKED))
+        add_share_and_store(1, slice(0, PICKED), nc.scalar)
+        share_of_lost_mass(2)
+        for i, cols in enumerate(pieces(TAPER)):
+            zero_the_dropped(2, cols)
+            add_share_and_store(2, cols, nc.sync if i % 2 == 0 else nc.scalar)

@@ -10,7 +10,7 @@ P = 128
 ROWS, CHANNELS, PICKED = 384, 4096, 2048
 BLOCKS = ROWS // P
 WHOLE = [PICKED]
-RISING = [128, 384, 512, 1024]
+RISING = [192, 320, 640, 896]
 TAPER = [832, 576, 384, 256]
 
 

import concourse.mybir as mybir

F32 = mybir.dt.float32
U16 = mybir.dt.uint16
MULT = mybir.AluOpType.mult
COPY = mybir.ActivationFunctionType.Copy
IDENTITY = mybir.ActivationFunctionType.Identity

P = 128
ROWS, CHANNELS, PICKED = 384, 4096, 2048
BLOCKS = ROWS // P
WHOLE = [PICKED]
RISING = [192, 320, 640, 896]
TAPER = [832, 576, 384, 256]


def pieces(widths):
    return [slice(sum(widths[:i]), sum(widths[: i + 1])) for i in range(len(widths))]


def tile_dropout_partial_binary_kernel(tc, x, keep, offs, out):
    nc = tc.nc
    with (
        tc.tile_pool(name="held", bufs=1) as held,
        tc.tile_pool(name="blocks", bufs=BLOCKS) as blocks,
    ):
        offsets = held.tile([P, PICKED // 16], U16, name="offsets")
        nc.sync.dma_start(offsets[:], offs)

        kept_masks = [blocks.tile([P, PICKED], F32, name="kept_mask") for b in range(BLOCKS)]
        dropped_masks = [blocks.tile([P, PICKED], F32, name="dropped_mask") for b in range(BLOCKS)]
        windows = [blocks.tile([P, CHANNELS], F32, name="window") for b in range(BLOCKS)]
        droppeds = [blocks.tile([P, PICKED], F32, name="dropped") for b in range(BLOCKS)]
        comps = [blocks.tile([P, 1], F32, name="comp") for b in range(BLOCKS)]
        results = [blocks.tile([P, PICKED], F32, name="result") for b in range(BLOCKS)]

        def load_window(b):
            nc.sync.dma_start(windows[b][:], x[b * P : (b + 1) * P, :])

        def load_masks(b, cuts):
            for cols in cuts:
                nc.sync.dma_start(kept_masks[b][:, cols], keep[b * P : (b + 1) * P, cols])
                nc.scalar.activation(dropped_masks[b][:, cols], kept_masks[b][:, cols], COPY, bias=1.0, scale=-1.0)

        def looked_up(b, cols):
            return windows[b][:].indirect(offsets[:, cols.start // 16 : cols.stop // 16])

        def share_of_lost_mass(b):
            nc.vector.tensor_tensor(droppeds[b][:], looked_up(b, slice(0, PICKED)), dropped_masks[b][:], MULT)
            nc.scalar.activation(droppeds[b][:], droppeds[b][:], COPY, scale=1.0 / PICKED, accum_out=comps[b][:])

        def zero_the_dropped(b, cols):
            nc.vector.tensor_tensor(results[b][:, cols], looked_up(b, cols), kept_masks[b][:, cols], MULT)

        def add_share_and_store(b, cols, store_queue):
            nc.scalar.activation(results[b][:, cols], results[b][:, cols], IDENTITY, bias=comps[b][:])
            store_queue.dma_start(out[b * P : (b + 1) * P, cols], results[b][:, cols])

        load_masks(0, pieces(RISING)[:1])
        load_window(0)
        load_masks(0, pieces(RISING)[1:])
        for b in range(1, BLOCKS):
            load_masks(b, pieces(WHOLE))
            load_window(b)

        for cols in pieces(RISING):
            zero_the_dropped(0, cols)
        share_of_lost_mass(0)
        add_share_and_store(0, slice(0, PICKED), nc.scalar)

        share_of_lost_mass(1)
        zero_the_dropped(1, slice(0, PICKED))
        add_share_and_store(1, slice(0, PICKED), nc.scalar)
        share_of_lost_mass(2)
        for i, cols in enumerate(pieces(TAPER)):
            zero_the_dropped(2, cols)
            add_share_and_store(2, cols, nc.sync if i % 2 == 0 else nc.scalar)
